import numpy as np
import ml_dtypes

BF16 = ml_dtypes.bfloat16


def bf(x):
    return np.asarray(x, np.float32).astype(BF16)


def f32(x):
    return np.asarray(x, np.float32)


def f64(x):
    return np.asarray(x).astype(np.float64)


def striped(idx):
    return np.tile(idx.reshape(-1, 16).T, (8, 1))


C, S, M, Q, T, N = 256, 2048, 128, 4, 512, 2048
BASE = 10000.0


def positional(length, width):
    place = np.arange(length, dtype=np.float32)[None, :]
    rate = np.exp(np.arange(0, width, 2, dtype=np.float32) * np.float32(-np.log(BASE) / width))[:, None]
    angle = f64(rate * place)
    pe = np.zeros((width, length))
    pe[0::2] = np.sin(angle)
    pe[1::2] = np.cos(angle)
    return pe


def setup_inputs():
    return {"table": f32(np.random.standard_normal((C, S))), "pos": f32(np.tile(positional(T, C), (1, Q))), "w": bf(np.random.standard_normal((C, M)) / np.sqrt(C)), "b": f32(0.1 * np.random.standard_normal((M, 1))), "offs": striped(np.random.permutation(np.tile(np.arange(S), 2))[:N])}


def reference(table, pos, w, b, offs):
    idx = offs[:16].T.reshape(-1)
    h = f64(table)[:, idx] + f64(pos)
    return f64(w).T @ h + f64(b)

@@ -1,0 +1,63 @@
+import concourse.mybir as mybir
+
+F32 = mybir.dt.float32
+BF16 = mybir.dt.bfloat16
+U16 = mybir.dt.uint16
+
+P = 128
+C, S, M, N = 256, 2048, 128, 2048
+BLOCKS = C // P
+PIECE = 512
+PIECES = N // PIECE
+PER_COLUMN = 16
+
+FLOPS = 2 * C * M * N
+
+
+def tile_sakt_kernel(tc, table, pos, w, b, offs, out):
+    nc = tc.nc
+    add = mybir.AluOpType.add
+    copy = mybir.ActivationFunctionType.Copy
+    identity = mybir.ActivationFunctionType.Identity
+
+    with (
+        tc.tile_pool(name="held", bufs=1) as held,
+        tc.tile_pool(name="ring", bufs=3) as ring,
+        tc.psum_pool(name="psum", bufs=1) as psum,
+    ):
+        offsets = held.tile([P, N // PER_COLUMN], U16, name="offsets")
+        nc.sync.dma_start(offsets[:], offs)
+        windows = [held.tile([P, S], F32, name=f"window{k}") for k in range(BLOCKS)]
+        pos_sb = [held.tile([P, N], F32, name=f"pos_sb{k}") for k in range(BLOCKS)]
+        for k in range(BLOCKS):
+            rows = slice(k * P, (k + 1) * P)
+            nc.sync.dma_start(windows[k][:], table[rows, :])
+            for j in range(PIECES):
+                cols = slice(j * PIECE, (j + 1) * PIECE)
+                nc.sync.dma_start(pos_sb[k][:, cols], pos[rows, cols])
+
+        w_sb = [held.tile([P, M], BF16, name=f"w_sb{k}") for k in range(BLOCKS)]
+        for k in range(BLOCKS):
+            nc.scalar.dma_start(w_sb[k][:], w[k * P : (k + 1) * P, :])
+        b_sb = held.tile([M, 1], F32, name="b_sb")
+        nc.scalar.dma_start(b_sb[:], b)
+
+        banks = [psum.tile([M, PIECE], F32, name=f"bank{j}") for j in range(PIECES)]
+
+        for k in range(BLOCKS):
+            for j in range(PIECES):
+                cols = slice(j * PIECE, (j + 1) * PIECE)
+                piece = offsets[:, j * PIECE // PER_COLUMN : (j + 1) * PIECE // PER_COLUMN]
+
+                h = ring.tile([P, PIECE], F32, name="h")
+                nc.vector.tensor_tensor(h[:], windows[k][:].indirect(piece), pos_sb[k][:, cols], add)
+
+                h_bf = ring.tile([P, PIECE], BF16, name="h_bf")
+                nc.scalar.activation(h_bf[:], h[:], copy)
+
+                nc.tensor.matmul(banks[j][:], w_sb[k][:], h_bf[:], start=(k == 0), stop=(k == BLOCKS - 1))
+
+                if k == BLOCKS - 1:
+                    y = ring.tile([M, PIECE], F32, name="y")
+                    nc.scalar.activation(y[:], banks[j][:], identity, bias=b_sb[:])
+                    nc.sync.dma_start(out[:, cols], y[:])

@@ -57,7 +57,12 @@ def tile_sakt_kernel(tc, table, pos, w, b, offs, out):
 
                 nc.tensor.matmul(banks[j][:], w_sb[k][:], h_bf[:], start=(k == 0), stop=(k == BLOCKS - 1))
 
-                if k == BLOCKS - 1:
+                if k == BLOCKS - 1 and j % 2 == 0:
                     y = ring.tile([M, PIECE], F32, name="y")
                     nc.scalar.activation(y[:], banks[j][:], identity, bias=b_sb[:])
                     nc.sync.dma_start(out[:, cols], y[:])
+
+        for j in range(1, PIECES, 2):
+            y = ring.tile([M, PIECE], F32, name="y")
+            nc.vector.tensor_scalar_add(y[:], banks[j][:], b_sb[:])
+            nc.sync.dma_start(out[:, j * PIECE : (j + 1) * PIECE], y[:])

@@ -7,9 +7,11 @@ U16 = mybir.dt.uint16
 P = 128
 C, S, M, N = 256, 2048, 128, 2048
 BLOCKS = C // P
-PIECE = 512
-PIECES = N // PIECE
 PER_COLUMN = 16
+
+WIDTHS = (512, 512, 512, 256, 128, 128)
+STARTS = tuple(sum(WIDTHS[:j]) for j in range(len(WIDTHS)))
+assert sum(WIDTHS) == N
 
 FLOPS = 2 * C * M * N
 
@@ -19,6 +21,7 @@ def tile_sakt_kernel(tc, table, pos, w, b, offs, out):
     add = mybir.AluOpType.add
     copy = mybir.ActivationFunctionType.Copy
     identity = mybir.ActivationFunctionType.Identity
+    pieces = tuple(enumerate(zip(STARTS, WIDTHS)))
 
     with (
         tc.tile_pool(name="held", bufs=1) as held,
@@ -32,8 +35,8 @@ def tile_sakt_kernel(tc, table, pos, w, b, offs, out):
         for k in range(BLOCKS):
             rows = slice(k * P, (k + 1) * P)
             nc.sync.dma_start(windows[k][:], table[rows, :])
-            for j in range(PIECES):
-                cols = slice(j * PIECE, (j + 1) * PIECE)
+            for j, (start, width) in pieces:
+                cols = slice(start, start + width)
                 nc.sync.dma_start(pos_sb[k][:, cols], pos[rows, cols])
 
         w_sb = [held.tile([P, M], BF16, name=f"w_sb{k}") for k in range(BLOCKS)]
@@ -42,27 +45,28 @@ def tile_sakt_kernel(tc, table, pos, w, b, offs, out):
         b_sb = held.tile([M, 1], F32, name="b_sb")
         nc.scalar.dma_start(b_sb[:], b)
 
-        banks = [psum.tile([M, PIECE], F32, name=f"bank{j}") for j in range(PIECES)]
+        banks = [psum.tile([M, width], F32, name=f"bank{j}") for j, (start, width) in pieces]
+        out_sb = held.tile([M, N], F32, name="out_sb")
 
         for k in range(BLOCKS):
-            for j in range(PIECES):
-                cols = slice(j * PIECE, (j + 1) * PIECE)
-                piece = offsets[:, j * PIECE // PER_COLUMN : (j + 1) * PIECE // PER_COLUMN]
+            for j, (start, width) in pieces:
+                cols = slice(start, start + width)
+                piece = offsets[:, start // PER_COLUMN : (start + width) // PER_COLUMN]
 
-                h = ring.tile([P, PIECE], F32, name="h")
+                h = ring.tile([P, width], F32, name="h")
                 nc.vector.tensor_tensor(h[:], windows[k][:].indirect(piece), pos_sb[k][:, cols], add)
 
-                h_bf = ring.tile([P, PIECE], BF16, name="h_bf")
+                h_bf = ring.tile([P, width], BF16, name="h_bf")
                 nc.scalar.activation(h_bf[:], h[:], copy)
 
                 nc.tensor.matmul(banks[j][:], w_sb[k][:], h_bf[:], start=(k == 0), stop=(k == BLOCKS - 1))
 
                 if k == BLOCKS - 1 and j % 2 == 0:
-                    y = ring.tile([M, PIECE], F32, name="y")
-                    nc.scalar.activation(y[:], banks[j][:], identity, bias=b_sb[:])
-                    nc.sync.dma_start(out[:, cols], y[:])
+                    nc.scalar.activation(out_sb[:, cols], banks[j][:], identity, bias=b_sb[:])
+                    nc.sync.dma_start(out[:, cols], out_sb[:, cols])
 
-        for j in range(1, PIECES, 2):
-            y = ring.tile([M, PIECE], F32, name="y")
-            nc.vector.tensor_scalar_add(y[:], banks[j][:], b_sb[:])
-            nc.sync.dma_start(out[:, j * PIECE : (j + 1) * PIECE], y[:])
+        for j, (start, width) in pieces:
+            if j % 2 == 1:
+                cols = slice(start, start + width)
+                nc.vector.tensor_scalar_add(out_sb[:, cols], banks[j][:], b_sb[:])
+                nc.sync.dma_start(out[:, cols], out_sb[:, cols])

@@ -8,12 +8,15 @@ P = 128
 C, S, M, N = 256, 2048, 128, 2048
 BLOCKS = C // P
 PER_COLUMN = 16
+BANK = 512
 
-WIDTHS = (512, 512, 512, 256, 128, 128)
-STARTS = tuple(sum(WIDTHS[:j]) for j in range(len(WIDTHS)))
-assert sum(WIDTHS) == N
+WIDTHS = ((BANK, BANK, BANK, BANK), (BANK, BANK, BANK, 256, 128, 128))
 
 FLOPS = 2 * C * M * N
+
+
+def spans(widths):
+    return tuple((sum(widths[:j]), widths[j]) for j in range(len(widths)))
 
 
 def tile_sakt_kernel(tc, table, pos, w, b, offs, out):
@@ -21,11 +24,10 @@ def tile_sakt_kernel(tc, table, pos, w, b, offs, out):
     add = mybir.AluOpType.add
     copy = mybir.ActivationFunctionType.Copy
     identity = mybir.ActivationFunctionType.Identity
-    pieces = tuple(enumerate(zip(STARTS, WIDTHS)))
 
     with (
         tc.tile_pool(name="held", bufs=1) as held,
-        tc.tile_pool(name="ring", bufs=3) as ring,
+        tc.tile_pool(name="ring", bufs=4) as ring,
         tc.psum_pool(name="psum", bufs=1) as psum,
     ):
         offsets = held.tile([P, N // PER_COLUMN], U16, name="offsets")
@@ -35,8 +37,8 @@ def tile_sakt_kernel(tc, table, pos, w, b, offs, out):
         for k in range(BLOCKS):
             rows = slice(k * P, (k + 1) * P)
             nc.sync.dma_start(windows[k][:], table[rows, :])
-            for j, (start, width) in pieces:
-                cols = slice(start, start + width)
+            for first in range(0, N, BANK):
+                cols = slice(first, first + BANK)
                 nc.sync.dma_start(pos_sb[k][:, cols], pos[rows, cols])
 
         w_sb = [held.tile([P, M], BF16, name=f"w_sb{k}") for k in range(BLOCKS)]
@@ -45,28 +47,36 @@ def tile_sakt_kernel(tc, table, pos, w, b, offs, out):
         b_sb = held.tile([M, 1], F32, name="b_sb")
         nc.scalar.dma_start(b_sb[:], b)
 
-        banks = [psum.tile([M, width], F32, name=f"bank{j}") for j, (start, width) in pieces]
+        sums = spans(WIDTHS[BLOCKS - 1])
+        banks = [psum.tile([M, width], F32, name=f"bank{j}") for j, (first, width) in enumerate(sums)]
         out_sb = held.tile([M, N], F32, name="out_sb")
 
         for k in range(BLOCKS):
-            for j, (start, width) in pieces:
-                cols = slice(start, start + width)
-                piece = offsets[:, start // PER_COLUMN : (start + width) // PER_COLUMN]
+            for start, length in spans(WIDTHS[k]):
+                piece = offsets[:, start // PER_COLUMN : (start + length) // PER_COLUMN]
 
-                h = ring.tile([P, width], F32, name="h")
-                nc.vector.tensor_tensor(h[:], windows[k][:].indirect(piece), pos_sb[k][:, cols], add)
+                h = ring.tile([P, length], F32, name="h")
+                nc.vector.tensor_tensor(
+                    h[:], windows[k][:].indirect(piece), pos_sb[k][:, start : start + length], add
+                )
 
-                h_bf = ring.tile([P, width], BF16, name="h_bf")
+                h_bf = ring.tile([P, length], BF16, name="h_bf")
                 nc.scalar.activation(h_bf[:], h[:], copy)
 
-                nc.tensor.matmul(banks[j][:], w_sb[k][:], h_bf[:], start=(k == 0), stop=(k == BLOCKS - 1))
+                for j, (first, width) in enumerate(sums):
+                    if start <= first < start + length:
+                        nc.tensor.matmul(
+                            banks[j][:],
+                            w_sb[k][:],
+                            h_bf[:, first - start : first - start + width],
+                            start=(k == 0),
+                            stop=(k == BLOCKS - 1),
+                        )
 
-                if k == BLOCKS - 1 and j % 2 == 0:
-                    nc.scalar.activation(out_sb[:, cols], banks[j][:], identity, bias=b_sb[:])
-                    nc.sync.dma_start(out[:, cols], out_sb[:, cols])
-
-        for j, (start, width) in pieces:
-            if j % 2 == 1:
-                cols = slice(start, start + width)
+        for j, (first, width) in enumerate(sums):
+            cols = slice(first, first + width)
+            if j % 2 == 0:
+                nc.scalar.activation(out_sb[:, cols], banks[j][:], identity, bias=b_sb[:])
+            else:
                 nc.vector.tensor_scalar_add(out_sb[:, cols], banks[j][:], b_sb[:])
-                nc.sync.dma_start(out[:, cols], out_sb[:, cols])
+            nc.sync.dma_start(out[:, cols], out_sb[:, cols])

@@ -75,8 +75,5 @@ def tile_sakt_kernel(tc, table, pos, w, b, offs, out):
 
         for j, (first, width) in enumerate(sums):
             cols = slice(first, first + width)
-            if j % 2 == 0:
-                nc.scalar.activation(out_sb[:, cols], banks[j][:], identity, bias=b_sb[:])
-            else:
-                nc.vector.tensor_scalar_add(out_sb[:, cols], banks[j][:], b_sb[:])
+            nc.scalar.activation(out_sb[:, cols], banks[j][:], identity, bias=b_sb[:])
             nc.sync.dma_start(out[:, cols], out_sb[:, cols])

@@ -10,7 +10,7 @@ BLOCKS = C // P
 PER_COLUMN = 16
 BANK = 512
 
-WIDTHS = ((BANK, BANK, BANK, BANK), (BANK, BANK, BANK, 256, 128, 128))
+WIDTHS = ((128, 384, BANK, BANK, BANK), (128, 384, BANK, BANK, 256, 128, 128))
 
 FLOPS = 2 * C * M * N
 
@@ -37,8 +37,8 @@ def tile_sakt_kernel(tc, table, pos, w, b, offs, out):
         for k in range(BLOCKS):
             rows = slice(k * P, (k + 1) * P)
             nc.sync.dma_start(windows[k][:], table[rows, :])
-            for first in range(0, N, BANK):
-                cols = slice(first, first + BANK)
+            for first, width in spans(WIDTHS[0]):
+                cols = slice(first, first + width)
                 nc.sync.dma_start(pos_sb[k][:, cols], pos[rows, cols])
 
         w_sb = [held.tile([P, M], BF16, name=f"w_sb{k}") for k in range(BLOCKS)]
@@ -75,5 +75,8 @@ def tile_sakt_kernel(tc, table, pos, w, b, offs, out):
 
         for j, (first, width) in enumerate(sums):
             cols = slice(first, first + width)
-            nc.scalar.activation(out_sb[:, cols], banks[j][:], identity, bias=b_sb[:])
+            if j % 2 == 0:
+                nc.scalar.activation(out_sb[:, cols], banks[j][:], identity, bias=b_sb[:])
+            else:
+                nc.vector.tensor_scalar_add(out_sb[:, cols], banks[j][:], b_sb[:])
             nc.sync.dma_start(out[:, cols], out_sb[:, cols])

@@ -6,6 +6,7 @@ U16 = mybir.dt.uint16
 
 P = 128
 C, S, M, N = 256, 2048, 128, 2048
+T = 512
 BLOCKS = C // P
 PER_COLUMN = 16
 BANK = 512
@@ -33,13 +34,14 @@ def tile_sakt_kernel(tc, table, pos, w, b, offs, out):
         offsets = held.tile([P, N // PER_COLUMN], U16, name="offsets")
         nc.sync.dma_start(offsets[:], offs)
         windows = [held.tile([P, S], F32, name=f"window{k}") for k in range(BLOCKS)]
-        pos_sb = [held.tile([P, N], F32, name=f"pos_sb{k}") for k in range(BLOCKS)]
+        pos_sb = [held.tile([P, T], F32, name=f"pos_sb{k}") for k in range(BLOCKS)]
         for k in range(BLOCKS):
             rows = slice(k * P, (k + 1) * P)
             nc.sync.dma_start(windows[k][:], table[rows, :])
             for first, width in spans(WIDTHS[0]):
-                cols = slice(first, first + width)
-                nc.sync.dma_start(pos_sb[k][:, cols], pos[rows, cols])
+                if first < T:
+                    cols = slice(first, first + width)
+                    nc.sync.dma_start(pos_sb[k][:, cols], pos[rows, cols])
 
         w_sb = [held.tile([P, M], BF16, name=f"w_sb{k}") for k in range(BLOCKS)]
         for k in range(BLOCKS):
@@ -57,7 +59,7 @@ def tile_sakt_kernel(tc, table, pos, w, b, offs, out):
 
                 h = ring.tile([P, length], F32, name="h")
                 nc.vector.tensor_tensor(
-                    h[:], windows[k][:].indirect(piece), pos_sb[k][:, start : start + length], add
+                    h[:], windows[k][:].indirect(piece), pos_sb[k][:, start % T : start % T + length], add
                 )
 
                 h_bf = ring.tile([P, length], BF16, name="h_bf")

@@ -6,12 +6,15 @@ U16 = mybir.dt.uint16
 
 P = 128
 C, S, M, N = 256, 2048, 128, 2048
-T = 512
+BANK = 512
 BLOCKS = C // P
 PER_COLUMN = 16
-BANK = 512
 
-WIDTHS = ((128, 384, BANK, BANK, BANK), (128, 384, BANK, BANK, 256, 128, 128))
+PIECES = ((BANK, BANK, 2 * BANK), (BANK, BANK, 256, 256, 256, 128, 128))
+
+FIRST = 128
+
+OWN = 3
 
 FLOPS = 2 * C * M * N
 
@@ -34,14 +37,13 @@ def tile_sakt_kernel(tc, table, pos, w, b, offs, out):
         offsets = held.tile([P, N // PER_COLUMN], U16, name="offsets")
         nc.sync.dma_start(offsets[:], offs)
         windows = [held.tile([P, S], F32, name=f"window{k}") for k in range(BLOCKS)]
-        pos_sb = [held.tile([P, T], F32, name=f"pos_sb{k}") for k in range(BLOCKS)]
+        pos_sb = [held.tile([P, N], F32, name=f"pos_sb{k}") for k in range(BLOCKS)]
         for k in range(BLOCKS):
             rows = slice(k * P, (k + 1) * P)
             nc.sync.dma_start(windows[k][:], table[rows, :])
-            for first, width in spans(WIDTHS[0]):
-                if first < T:
-                    cols = slice(first, first + width)
-                    nc.sync.dma_start(pos_sb[k][:, cols], pos[rows, cols])
+            for first, width in spans((FIRST, PIECES[0][0] - FIRST) + PIECES[0][1:]):
+                cols = slice(first, first + width)
+                nc.sync.dma_start(pos_sb[k][:, cols], pos[rows, cols])
 
         w_sb = [held.tile([P, M], BF16, name=f"w_sb{k}") for k in range(BLOCKS)]
         for k in range(BLOCKS):
@@ -49,21 +51,28 @@ def tile_sakt_kernel(tc, table, pos, w, b, offs, out):
         b_sb = held.tile([M, 1], F32, name="b_sb")
         nc.scalar.dma_start(b_sb[:], b)
 
-        sums = spans(WIDTHS[BLOCKS - 1])
+        sums = spans(PIECES[BLOCKS - 1])
         banks = [psum.tile([M, width], F32, name=f"bank{j}") for j, (first, width) in enumerate(sums)]
         out_sb = held.tile([M, N], F32, name="out_sb")
 
         for k in range(BLOCKS):
-            for start, length in spans(WIDTHS[k]):
-                piece = offsets[:, start // PER_COLUMN : (start + length) // PER_COLUMN]
-
+            for i, (start, length) in enumerate(spans(PIECES[k])):
                 h = ring.tile([P, length], F32, name="h")
-                nc.vector.tensor_tensor(
-                    h[:], windows[k][:].indirect(piece), pos_sb[k][:, start % T : start % T + length], add
-                )
+                parts = (FIRST, length - FIRST) if (k == 0 and i == 0) else (length,)
+                for at, n in spans(parts):
+                    entries = offsets[:, (start + at) // PER_COLUMN : (start + at + n) // PER_COLUMN]
+                    nc.vector.tensor_tensor(
+                        h[:, at : at + n],
+                        windows[k][:].indirect(entries),
+                        pos_sb[k][:, start + at : start + at + n],
+                        add,
+                    )
 
                 h_bf = ring.tile([P, length], BF16, name="h_bf")
-                nc.scalar.activation(h_bf[:], h[:], copy)
+                if k == BLOCKS - 1 and i >= len(PIECES[k]) - OWN:
+                    nc.vector.tensor_copy(h_bf[:], h[:])
+                else:
+                    nc.scalar.activation(h_bf[:], h[:], copy)
 
                 for j, (first, width) in enumerate(sums):
                     if start <= first < start + length:
@@ -77,8 +86,8 @@ def tile_sakt_kernel(tc, table, pos, w, b, offs, out):
 
         for j, (first, width) in enumerate(sums):
             cols = slice(first, first + width)
-            if j % 2 == 0:
-                nc.scalar.activation(out_sb[:, cols], banks[j][:], identity, bias=b_sb[:])
-            else:
+            if j >= len(sums) - OWN:
                 nc.vector.tensor_scalar_add(out_sb[:, cols], banks[j][:], b_sb[:])
+            else:
+                nc.scalar.activation(out_sb[:, cols], banks[j][:], identity, bias=b_sb[:])
             nc.sync.dma_start(out[:, cols], out_sb[:, cols])

@@ -10,17 +10,20 @@ BANK = 512
 BLOCKS = C // P
 PER_COLUMN = 16
 
-PIECES = ((BANK, BANK, 2 * BANK), (BANK, BANK, 256, 256, 256, 128, 128))
+PIECES = ((BANK, BANK, 2 * BANK), (BANK, BANK, 384, 256, 256, 128))
 
 FIRST = 128
-
-OWN = 3
 
 FLOPS = 2 * C * M * N
 
 
 def spans(widths):
     return tuple((sum(widths[:j]), widths[j]) for j in range(len(widths)))
+
+
+def parts_of(k, i):
+    length = PIECES[k][i]
+    return (FIRST, length - FIRST) if (k == 0 and i == 0) else (length,)
 
 
 def tile_sakt_kernel(tc, table, pos, w, b, offs, out):
@@ -41,9 +44,10 @@ def tile_sakt_kernel(tc, table, pos, w, b, offs, out):
         for k in range(BLOCKS):
             rows = slice(k * P, (k + 1) * P)
             nc.sync.dma_start(windows[k][:], table[rows, :])
-            for first, width in spans((FIRST, PIECES[0][0] - FIRST) + PIECES[0][1:]):
-                cols = slice(first, first + width)
-                nc.sync.dma_start(pos_sb[k][:, cols], pos[rows, cols])
+            for i, (start, length) in enumerate(spans(PIECES[k])):
+                for at, n in spans(parts_of(k, i)):
+                    cols = slice(start + at, start + at + n)
+                    nc.sync.dma_start(pos_sb[k][:, cols], pos[rows, cols])
 
         w_sb = [held.tile([P, M], BF16, name=f"w_sb{k}") for k in range(BLOCKS)]
         for k in range(BLOCKS):
@@ -58,8 +62,7 @@ def tile_sakt_kernel(tc, table, pos, w, b, offs, out):
         for k in range(BLOCKS):
             for i, (start, length) in enumerate(spans(PIECES[k])):
                 h = ring.tile([P, length], F32, name="h")
-                parts = (FIRST, length - FIRST) if (k == 0 and i == 0) else (length,)
-                for at, n in spans(parts):
+                for at, n in spans(parts_of(k, i)):
                     entries = offsets[:, (start + at) // PER_COLUMN : (start + at + n) // PER_COLUMN]
                     nc.vector.tensor_tensor(
                         h[:, at : at + n],
@@ -69,10 +72,7 @@ def tile_sakt_kernel(tc, table, pos, w, b, offs, out):
                     )
 
                 h_bf = ring.tile([P, length], BF16, name="h_bf")
-                if k == BLOCKS - 1 and i >= len(PIECES[k]) - OWN:
-                    nc.vector.tensor_copy(h_bf[:], h[:])
-                else:
-                    nc.scalar.activation(h_bf[:], h[:], copy)
+                nc.scalar.activation(h_bf[:], h[:], copy)
 
                 for j, (first, width) in enumerate(sums):
                     if start <= first < start + length:
@@ -86,7 +86,7 @@ def tile_sakt_kernel(tc, table, pos, w, b, offs, out):
 
         for j, (first, width) in enumerate(sums):
             cols = slice(first, first + width)
-            if j >= len(sums) - OWN:
+            if j % 2 == 1:
                 nc.vector.tensor_scalar_add(out_sb[:, cols], banks[j][:], b_sb[:])
             else:
                 nc.scalar.activation(out_sb[:, cols], banks[j][:], identity, bias=b_sb[:])

@@ -23,7 +23,7 @@ def spans(widths):
 
 def parts_of(k, i):
     length = PIECES[k][i]
-    return (FIRST, length - FIRST) if (k == 0 and i == 0) else (length,)
+    return (FIRST, length - FIRST) if i == 0 else (length,)
 
 
 def tile_sakt_kernel(tc, table, pos, w, b, offs, out):

@@ -72,7 +72,10 @@ def tile_sakt_kernel(tc, table, pos, w, b, offs, out):
                     )
 
                 h_bf = ring.tile([P, length], BF16, name="h_bf")
-                nc.scalar.activation(h_bf[:], h[:], copy)
+                if k == BLOCKS - 1 and i >= len(PIECES[k]) - 2:
+                    nc.vector.tensor_copy(h_bf[:], h[:])
+                else:
+                    nc.scalar.activation(h_bf[:], h[:], copy)
 
                 for j, (first, width) in enumerate(sums):
                     if start <= first < start + length:

@@ -43,11 +43,13 @@ def tile_sakt_kernel(tc, table, pos, w, b, offs, out):
         pos_sb = [held.tile([P, N], F32, name=f"pos_sb{k}") for k in range(BLOCKS)]
         for k in range(BLOCKS):
             rows = slice(k * P, (k + 1) * P)
+            nc.sync.dma_start(pos_sb[k][:, :FIRST], pos[rows, :FIRST])
             nc.sync.dma_start(windows[k][:], table[rows, :])
             for i, (start, length) in enumerate(spans(PIECES[k])):
                 for at, n in spans(parts_of(k, i)):
-                    cols = slice(start + at, start + at + n)
-                    nc.sync.dma_start(pos_sb[k][:, cols], pos[rows, cols])
+                    if start + at > 0:
+                        cols = slice(start + at, start + at + n)
+                        nc.sync.dma_start(pos_sb[k][:, cols], pos[rows, cols])
 
         w_sb = [held.tile([P, M], BF16, name=f"w_sb{k}") for k in range(BLOCKS)]
         for k in range(BLOCKS):

@@ -60,6 +60,16 @@ def tile_sakt_kernel(tc, table, pos, w, b, offs, out):
         sums = spans(PIECES[BLOCKS - 1])
         banks = [psum.tile([M, width], F32, name=f"bank{j}") for j, (first, width) in enumerate(sums)]
         out_sb = held.tile([M, N], F32, name="out_sb")
+        of_scalar = len(sums) // 2
+
+        def evacuate(j):
+            first, width = sums[j]
+            cols = slice(first, first + width)
+            if j < of_scalar:
+                nc.scalar.activation(out_sb[:, cols], banks[j][:], identity, bias=b_sb[:])
+            else:
+                nc.vector.tensor_scalar_add(out_sb[:, cols], banks[j][:], b_sb[:])
+            nc.sync.dma_start(out[:, cols], out_sb[:, cols])
 
         for k in range(BLOCKS):
             for i, (start, length) in enumerate(spans(PIECES[k])):
@@ -77,7 +87,9 @@ def tile_sakt_kernel(tc, table, pos, w, b, offs, out):
                 if k == BLOCKS - 1 and i >= len(PIECES[k]) - 2:
                     nc.vector.tensor_copy(h_bf[:], h[:])
                 else:
-                    nc.scalar.activation(h_bf[:], h[:], copy)
+                    for at in range(0, length, BANK):
+                        part = slice(at, min(at + BANK, length))
+                        nc.scalar.activation(h_bf[:, part], h[:, part], copy)
 
                 for j, (first, width) in enumerate(sums):
                     if start <= first < start + length:
@@ -89,10 +101,8 @@ def tile_sakt_kernel(tc, table, pos, w, b, offs, out):
                             stop=(k == BLOCKS - 1),
                         )
 
-        for j, (first, width) in enumerate(sums):
-            cols = slice(first, first + width)
-            if j % 2 == 1:
-                nc.vector.tensor_scalar_add(out_sb[:, cols], banks[j][:], b_sb[:])
-            else:
-                nc.scalar.activation(out_sb[:, cols], banks[j][:], identity, bias=b_sb[:])
-            nc.sync.dma_start(out[:, cols], out_sb[:, cols])
+                if k == BLOCKS - 1 and 1 <= i <= of_scalar:
+                    evacuate(i - 1)
+
+        for j in range(of_scalar, len(sums)):
+            evacuate(j)

@@ -60,7 +60,7 @@ def tile_sakt_kernel(tc, table, pos, w, b, offs, out):
         sums = spans(PIECES[BLOCKS - 1])
         banks = [psum.tile([M, width], F32, name=f"bank{j}") for j, (first, width) in enumerate(sums)]
         out_sb = held.tile([M, N], F32, name="out_sb")
-        of_scalar = len(sums) // 2
+        of_scalar = len(sums) - 2
 
         def evacuate(j):
             first, width = sums[j]

@@ -6,24 +6,17 @@ U16 = mybir.dt.uint16
 
 P = 128
 C, S, M, N = 256, 2048, 128, 2048
-BANK = 512
+STEPS = 512
 BLOCKS = C // P
 PER_COLUMN = 16
 
-PIECES = ((BANK, BANK, 2 * BANK), (BANK, BANK, 384, 256, 256, 128))
-
 FIRST = 128
 
+SUMS = ((0, 512), (512, 512), (1024, 512), (1536, 256), (1792, 128), (1920, 128))
+
+LEAD = 3
+
 FLOPS = 2 * C * M * N
-
-
-def spans(widths):
-    return tuple((sum(widths[:j]), widths[j]) for j in range(len(widths)))
-
-
-def parts_of(k, i):
-    length = PIECES[k][i]
-    return (FIRST, length - FIRST) if i == 0 else (length,)
 
 
 def tile_sakt_kernel(tc, table, pos, w, b, offs, out):
@@ -38,18 +31,14 @@ def tile_sakt_kernel(tc, table, pos, w, b, offs, out):
         tc.psum_pool(name="psum", bufs=1) as psum,
     ):
         offsets = held.tile([P, N // PER_COLUMN], U16, name="offsets")
-        nc.sync.dma_start(offsets[:], offs)
         windows = [held.tile([P, S], F32, name=f"window{k}") for k in range(BLOCKS)]
-        pos_sb = [held.tile([P, N], F32, name=f"pos_sb{k}") for k in range(BLOCKS)]
-        for k in range(BLOCKS):
-            rows = slice(k * P, (k + 1) * P)
-            nc.sync.dma_start(pos_sb[k][:, :FIRST], pos[rows, :FIRST])
-            nc.sync.dma_start(windows[k][:], table[rows, :])
-            for i, (start, length) in enumerate(spans(PIECES[k])):
-                for at, n in spans(parts_of(k, i)):
-                    if start + at > 0:
-                        cols = slice(start + at, start + at + n)
-                        nc.sync.dma_start(pos_sb[k][:, cols], pos[rows, cols])
+        pos_sb = [held.tile([P, STEPS], F32, name=f"pos_sb{k}") for k in range(BLOCKS)]
+        nc.sync.dma_start(offsets[:], offs)
+        nc.sync.dma_start(pos_sb[0][:, :FIRST], pos[:P, :FIRST])
+        nc.sync.dma_start(windows[0][:], table[:P, :])
+        nc.sync.dma_start(pos_sb[0][:, FIRST:], pos[:P, FIRST:STEPS])
+        nc.sync.dma_start(pos_sb[1][:], pos[P:, :STEPS])
+        nc.sync.dma_start(windows[1][:], table[P:, :])
 
         w_sb = [held.tile([P, M], BF16, name=f"w_sb{k}") for k in range(BLOCKS)]
         for k in range(BLOCKS):
@@ -57,13 +46,47 @@ def tile_sakt_kernel(tc, table, pos, w, b, offs, out):
         b_sb = held.tile([M, 1], F32, name="b_sb")
         nc.scalar.dma_start(b_sb[:], b)
 
-        sums = spans(PIECES[BLOCKS - 1])
-        banks = [psum.tile([M, width], F32, name=f"bank{j}") for j, (first, width) in enumerate(sums)]
+        banks = [psum.tile([M, width], F32, name=f"bank{j}") for j, (first, width) in enumerate(SUMS)]
         out_sb = held.tile([M, N], F32, name="out_sb")
-        of_scalar = len(sums) - 2
+        of_scalar = len(SUMS) - 2
+
+        def look_up(k, start, lengths):
+            h = ring.tile([P, sum(lengths)], F32, name="h")
+            at = 0
+            for n in lengths:
+                entries = offsets[:, (start + at) // PER_COLUMN : (start + at + n) // PER_COLUMN]
+                step = (start + at) % STEPS
+                nc.vector.tensor_tensor(
+                    h[:, at : at + n],
+                    windows[k][:].indirect(entries),
+                    pos_sb[k][:, step : step + n],
+                    add,
+                )
+                at += n
+            return h
+
+        def block0(q):
+            start = q * STEPS
+            h = look_up(0, start, (FIRST, STEPS - FIRST) if q == 0 else (STEPS,))
+            h_bf = ring.tile([P, STEPS], BF16, name="h_bf")
+            nc.scalar.activation(h_bf[:], h[:], copy)
+            for j, (first, width) in enumerate(SUMS):
+                if start <= first < start + STEPS:
+                    moving = h_bf[:, first - start : first - start + width]
+                    nc.tensor.matmul(banks[j][:], w_sb[0][:], moving, start=True, stop=False)
+
+        def block1(j):
+            first, width = SUMS[j]
+            h = look_up(1, first, (width,))
+            h_bf = ring.tile([P, width], BF16, name="h_bf")
+            if j < of_scalar:
+                nc.scalar.activation(h_bf[:], h[:], copy)
+            else:
+                nc.vector.tensor_copy(h_bf[:], h[:])
+            nc.tensor.matmul(banks[j][:], w_sb[1][:], h_bf[:], start=False, stop=True)
 
         def evacuate(j):
-            first, width = sums[j]
+            first, width = SUMS[j]
             cols = slice(first, first + width)
             if j < of_scalar:
                 nc.scalar.activation(out_sb[:, cols], banks[j][:], identity, bias=b_sb[:])
@@ -71,38 +94,13 @@ def tile_sakt_kernel(tc, table, pos, w, b, offs, out):
                 nc.vector.tensor_scalar_add(out_sb[:, cols], banks[j][:], b_sb[:])
             nc.sync.dma_start(out[:, cols], out_sb[:, cols])
 
-        for k in range(BLOCKS):
-            for i, (start, length) in enumerate(spans(PIECES[k])):
-                h = ring.tile([P, length], F32, name="h")
-                for at, n in spans(parts_of(k, i)):
-                    entries = offsets[:, (start + at) // PER_COLUMN : (start + at + n) // PER_COLUMN]
-                    nc.vector.tensor_tensor(
-                        h[:, at : at + n],
-                        windows[k][:].indirect(entries),
-                        pos_sb[k][:, start + at : start + at + n],
-                        add,
-                    )
-
-                h_bf = ring.tile([P, length], BF16, name="h_bf")
-                if k == BLOCKS - 1 and i >= len(PIECES[k]) - 2:
-                    nc.vector.tensor_copy(h_bf[:], h[:])
-                else:
-                    for at in range(0, length, BANK):
-                        part = slice(at, min(at + BANK, length))
-                        nc.scalar.activation(h_bf[:, part], h[:, part], copy)
-
-                for j, (first, width) in enumerate(sums):
-                    if start <= first < start + length:
-                        nc.tensor.matmul(
-                            banks[j][:],
-                            w_sb[k][:],
-                            h_bf[:, first - start : first - start + width],
-                            start=(k == 0),
-                            stop=(k == BLOCKS - 1),
-                        )
-
-                if k == BLOCKS - 1 and 1 <= i <= of_scalar:
-                    evacuate(i - 1)
-
-        for j in range(of_scalar, len(sums)):
+        for q in range(LEAD):
+            block0(q)
+        for j in range(len(SUMS)):
+            block1(j)
+            if LEAD + j < N // STEPS:
+                block0(LEAD + j)
+            if 1 <= j <= of_scalar:
+                evacuate(j - 1)
+        for j in range(of_scalar, len(SUMS)):
             evacuate(j)

@@ -39,10 +39,10 @@ def tile_sakt_kernel(tc, table, pos, w, b, offs, out):
         nc.sync.dma_start(pos_sb[0][:, FIRST:], pos[:P, FIRST:STEPS])
         nc.sync.dma_start(pos_sb[1][:], pos[P:, :STEPS])
         nc.sync.dma_start(windows[1][:], table[P:, :])
-
         w_sb = [held.tile([P, M], BF16, name=f"w_sb{k}") for k in range(BLOCKS)]
         for k in range(BLOCKS):
-            nc.scalar.dma_start(w_sb[k][:], w[k * P : (k + 1) * P, :])
+            nc.sync.dma_start(w_sb[k][:], w[k * P : (k + 1) * P, :])
+
         b_sb = held.tile([M, 1], F32, name="b_sb")
         nc.scalar.dma_start(b_sb[:], b)
 

@@ -42,9 +42,8 @@ def tile_sakt_kernel(tc, table, pos, w, b, offs, out):
         w_sb = [held.tile([P, M], BF16, name=f"w_sb{k}") for k in range(BLOCKS)]
         for k in range(BLOCKS):
             nc.sync.dma_start(w_sb[k][:], w[k * P : (k + 1) * P, :])
-
         b_sb = held.tile([M, 1], F32, name="b_sb")
-        nc.scalar.dma_start(b_sb[:], b)
+        nc.sync.dma_start(b_sb[:], b)
 
         banks = [psum.tile([M, width], F32, name=f"bank{j}") for j, (first, width) in enumerate(SUMS)]
         out_sb = held.tile([M, N], F32, name="out_sb")

@@ -35,7 +35,8 @@ def tile_sakt_kernel(tc, table, pos, w, b, offs, out):
         pos_sb = [held.tile([P, STEPS], F32, name=f"pos_sb{k}") for k in range(BLOCKS)]
         nc.sync.dma_start(offsets[:], offs)
         nc.sync.dma_start(pos_sb[0][:, :FIRST], pos[:P, :FIRST])
-        nc.sync.dma_start(windows[0][:], table[:P, :])
+        nc.sync.dma_start(windows[0][:, : S // 2], table[:P, : S // 2])
+        nc.scalar.dma_start(windows[0][:, S // 2 :], table[:P, S // 2 :])
         nc.sync.dma_start(pos_sb[0][:, FIRST:], pos[:P, FIRST:STEPS])
         nc.sync.dma_start(pos_sb[1][:], pos[P:, :STEPS])
         nc.sync.dma_start(windows[1][:], table[P:, :])

import concourse.mybir as mybir

F32 = mybir.dt.float32
BF16 = mybir.dt.bfloat16
U16 = mybir.dt.uint16

P = 128
C, S, M, N = 256, 2048, 128, 2048
STEPS = 512
BLOCKS = C // P
PER_COLUMN = 16

FIRST = 128

SUMS = ((0, 512), (512, 512), (1024, 512), (1536, 256), (1792, 128), (1920, 128))

LEAD = 3

FLOPS = 2 * C * M * N


def tile_sakt_kernel(tc, table, pos, w, b, offs, out):
    nc = tc.nc
    add = mybir.AluOpType.add
    copy = mybir.ActivationFunctionType.Copy
    identity = mybir.ActivationFunctionType.Identity

    with (
        tc.tile_pool(name="held", bufs=1) as held,
        tc.tile_pool(name="ring", bufs=4) as ring,
        tc.psum_pool(name="psum", bufs=1) as psum,
    ):
        offsets = held.tile([P, N // PER_COLUMN], U16, name="offsets")
        windows = [held.tile([P, S], F32, name=f"window{k}") for k in range(BLOCKS)]
        pos_sb = [held.tile([P, STEPS], F32, name=f"pos_sb{k}") for k in range(BLOCKS)]
        nc.sync.dma_start(offsets[:], offs)
        nc.sync.dma_start(pos_sb[0][:, :FIRST], pos[:P, :FIRST])
        nc.sync.dma_start(windows[0][:, : S // 2], table[:P, : S // 2])
        nc.scalar.dma_start(windows[0][:, S // 2 :], table[:P, S // 2 :])
        nc.sync.dma_start(pos_sb[0][:, FIRST:], pos[:P, FIRST:STEPS])
        nc.sync.dma_start(pos_sb[1][:], pos[P:, :STEPS])
        nc.sync.dma_start(windows[1][:], table[P:, :])
        w_sb = [held.tile([P, M], BF16, name=f"w_sb{k}") for k in range(BLOCKS)]
        for k in range(BLOCKS):
            nc.sync.dma_start(w_sb[k][:], w[k * P : (k + 1) * P, :])
        b_sb = held.tile([M, 1], F32, name="b_sb")
        nc.sync.dma_start(b_sb[:], b)

        banks = [psum.tile([M, width], F32, name=f"bank{j}") for j, (first, width) in enumerate(SUMS)]
        out_sb = held.tile([M, N], F32, name="out_sb")
        of_scalar = len(SUMS) - 2

        def look_up(k, start, lengths):
            h = ring.tile([P, sum(lengths)], F32, name="h")
            at = 0
            for n in lengths:
                entries = offsets[:, (start + at) // PER_COLUMN : (start + at + n) // PER_COLUMN]
                step = (start + at) % STEPS
                nc.vector.tensor_tensor(
                    h[:, at : at + n],
                    windows[k][:].indirect(entries),
                    pos_sb[k][:, step : step + n],
                    add,
                )
                at += n
            return h

        def block0(q):
            start = q * STEPS
            h = look_up(0, start, (FIRST, STEPS - FIRST) if q == 0 else (STEPS,))
            h_bf = ring.tile([P, STEPS], BF16, name="h_bf")
            nc.scalar.activation(h_bf[:], h[:], copy)
            for j, (first, width) in enumerate(SUMS):
                if start <= first < start + STEPS:
                    moving = h_bf[:, first - start : first - start + width]
                    nc.tensor.matmul(banks[j][:], w_sb[0][:], moving, start=True, stop=False)

        def block1(j):
            first, width = SUMS[j]
            h = look_up(1, first, (width,))
            h_bf = ring.tile([P, width], BF16, name="h_bf")
            if j < of_scalar:
                nc.scalar.activation(h_bf[:], h[:], copy)
            else:
                nc.vector.tensor_copy(h_bf[:], h[:])
            nc.tensor.matmul(banks[j][:], w_sb[1][:], h_bf[:], start=False, stop=True)

        def evacuate(j):
            first, width = SUMS[j]
            cols = slice(first, first + width)
            if j < of_scalar:
                nc.scalar.activation(out_sb[:, cols], banks[j][:], identity, bias=b_sb[:])
            else:
                nc.vector.tensor_scalar_add(out_sb[:, cols], banks[j][:], b_sb[:])
            nc.sync.dma_start(out[:, cols], out_sb[:, cols])

        for q in range(LEAD):
            block0(q)
        for j in range(len(SUMS)):
            block1(j)
            if LEAD + j < N // STEPS:
                block0(LEAD + j)
            if 1 <= j <= of_scalar:
                evacuate(j - 1)
        for j in range(of_scalar, len(SUMS)):
            evacuate(j)
